import numpy as np
import ml_dtypes


def mxq(x, axis, fmt="e4m3"):
    dtype, down = {"e4m3": (ml_dtypes.float8_e4m3fn, 7), "e5m2": (ml_dtypes.float8_e5m2, 14)}[fmt]
    v = np.moveaxis(np.asarray(x, np.float32).astype(ml_dtypes.bfloat16).astype(np.float64), axis, -1)
    blocks = v.reshape(v.shape[:-1] + (-1, 32))
    amax = np.abs(blocks).max(-1, keepdims=True)
    byte = np.maximum(np.where(amax > 0, np.frexp(amax)[1] - 1 + 127, 0) - down, 1)
    scale = np.exp2(byte - 127.0)
    codes = (blocks / scale).astype(np.float32).astype(dtype).astype(np.float64)
    return np.moveaxis((codes * scale).reshape(v.shape), -1, axis)


WIDE = False


def mx_kscale(k):
    if not WIDE:
        return np.ones(k)
    levels = np.array([10, -10, 5, -5, 0])
    if k % 512:
        return np.exp2(np.random.permutation(np.resize(levels, k // 32))).repeat(32)
    a = np.empty((k // 512, 16))
    for p in range(k // 512):
        a[p, :8] = np.random.permutation(np.resize(levels, 8))
        for g in range(8):
            far = levels[np.abs(levels - a[p, g]) >= 10]
            a[p, g + 8] = far[np.random.randint(len(far))]
    return np.exp2(a.ravel()).repeat(32)


BF16 = ml_dtypes.bfloat16


def bf(x):
    return np.asarray(x, np.float32).astype(BF16)


def f64(x):
    return np.asarray(x).astype(np.float64)


B, T, H, HD = 2, 256, 16, 128
D = H * HD
HALF = HD // 2
ROPE_BASE = 10000.0


def to_heads(t):
    return t.reshape(B, T, H, HD).transpose(0, 2, 1, 3)


def rotate(t, cos, sin):
    t1, t2 = t[..., :HALF], t[..., HALF:]
    c = cos[None, None, :, :]
    s = sin[None, None, :, :]
    return np.concatenate([t1 * c - t2 * s, t1 * s + t2 * c], axis=-1)


def draw0():
    s = mx_kscale(D)
    inv_freq = 1.0 / (ROPE_BASE ** (np.arange(0, HD, 2) / HD))
    ang = np.arange(T)[:, None] * inv_freq[None, :]
    return {"x": bf(np.random.standard_normal((B, T, D)) * s),
            "Wqk": bf(np.random.standard_normal((2 * D, D)) * D ** -0.5 / s[None, :]),
            "bqk": bf(np.random.standard_normal(2 * D) * 0.3),
            "cos": bf(np.cos(ang)),
            "sin": bf(np.sin(ang))}


def core(x, Wqk, bqk, cos, sin):
    qk = (mxq(f64(x), 2, "e4m3") @ mxq(f64(Wqk), 1, "e4m3").T) + f64(bqk)
    q, k = np.split(qk, 2, axis=-1)
    q, k = to_heads(q), to_heads(k)
    return rotate(q, f64(cos), f64(sin)), rotate(k, f64(cos), f64(sin))


def e4m3fn_bytes(y):
    return np.clip(np.asarray(y, np.float64), -448.0, 448.0).astype(np.float32).astype(ml_dtypes.float8_e4m3fn).view(np.uint8)


def e4m3fn_values(b):
    return np.asarray(b, np.uint8).view(ml_dtypes.float8_e4m3fn).astype(np.float64)


def setup_inputs():
    d = draw0()
    x0 = np.asarray(d['Wqk']).astype(np.float64)
    s = (np.max(np.abs(x0), axis=(0,), keepdims=True) / 448.0).astype(np.float32)
    out = {}
    for k, v in d.items():
        if k == 'Wqk':
            out['Wqk_bytes'] = e4m3fn_bytes(x0 / s.astype(np.float64))
            out['Wqk_scale'] = s
        else:
            out[k] = v
    return out


def reference(x, Wqk_bytes, Wqk_scale, bqk, cos, sin):
    return core(x, e4m3fn_values(Wqk_bytes) * Wqk_scale.astype(np.float64), bqk, cos, sin)

@@ -1,0 +1,304 @@
+from contextlib import ExitStack
+
+import concourse.mybir as mybir
+from concourse.masks import make_identity
+
+F32 = mybir.dt.float32
+BF16 = mybir.dt.bfloat16
+U32 = mybir.dt.uint32
+U8 = mybir.dt.uint8
+FP8 = mybir.dt.float8_e4m3fn
+FP8X4 = mybir.dt.float8_e4m3fn_x4
+ALU = mybir.AluOpType
+ACT = mybir.ActivationFunctionType
+
+P = 128
+K = 2048
+PASSES = 4
+NSTEP = 16
+FLOPS = 2 * 512 * 4096 * 2048
+
+ON_GPSIMD = tuple((k, jj) for k in range(NSTEP - 1) for jj in range(2))
+
+
+def tile_selfattention_pa_kernel(tc, x, Wqk_bytes, Wqk_scale, bqk, cos, sin, out_0, out_1):
+    nc = tc.nc
+    with ExitStack() as ctx:
+        const = ctx.enter_context(tc.tile_pool(name="const", bufs=1))
+        wraw = ctx.enter_context(tc.tile_pool(name="wraw", bufs=NSTEP))
+        wbp = ctx.enter_context(tc.tile_pool(name="wbp", bufs=3))
+        wgp = ctx.enter_context(tc.tile_pool(name="wgp", bufs=2))
+        wcp = ctx.enter_context(tc.tile_pool(name="wcp", bufs=2))
+        uvp = ctx.enter_context(tc.tile_pool(name="uvp", bufs=6))
+        ytp = ctx.enter_context(tc.tile_pool(name="ytp", bufs=3))
+        outp = ctx.enter_context(tc.tile_pool(name="outp", bufs=4))
+        tpp = ctx.enter_context(tc.psum_pool(name="tpp", bufs=4))
+        accp = ctx.enter_context(tc.psum_pool(name="accp", bufs=2))
+        backp = ctx.enter_context(tc.psum_pool(name="backp", bufs=2))
+
+        wbys = {}
+        wbs = {}
+        wgs = {}
+        codes = {}
+        accs = {}
+        uvs = {}
+        backs = {}
+        outs = {}
+
+        x_sb = {}
+        for b in range(2):
+            for half in range(2):
+                x_sb[(b, half)] = const.tile([P, 2, 1024], BF16, name="x_sb%d%d" % (b, half))
+        sc4 = const.tile([P, PASSES, 4], F32, name="sc4")
+        cos_sb = const.tile([P, 2, 64], BF16, name="cos_sb")
+        sin_sb = const.tile([P, 2, 64], BF16, name="sin_sb")
+        brow_bf = const.tile([32, P], BF16, name="brow_bf")
+        brow = const.tile([P, P], F32, name="brow")
+        biasc = const.tile([P, 32], F32, name="biasc")
+        ident = const.tile([P, P], F32, name="ident")
+        perm = const.tile([P, P], F32, name="perm")
+        nat = const.tile([P, 2, 2, 2, 64], F32, name="nat")
+        tabs = const.tile([P, 2, 256], F32, name="tabs")
+        xg = const.tile([P, PASSES, 512, 4], BF16, name="xg", align_bytes=64)
+        xc = const.tile([P, PASSES, 512], U32, name="xc", align_bytes=64)
+        xs = const.tile([P, PASSES, 512], U8, name="xs", align_bytes=64)
+
+        def load_x(b, half):
+            nc.sync.dma_start(
+                out=x_sb[(b, half)][:],
+                in_=x[b].rearrange("(p e) k -> p e k", e=2)[:, :, 1024 * half : 1024 * (half + 1)],
+            )
+
+        def load_w(k):
+            wby = wraw.tile([P, 2, K], U8, name="wby")
+            nc.sync.dma_start(out=wby[:], in_=Wqk_bytes[256 * k : 256 * (k + 1), :].rearrange("(j p) k -> p j k", p=P))
+            wbys[k] = wby
+
+        make_identity(nc, ident[:])
+
+        def casts(k):
+            wb = wbp.tile([P, 2, K], BF16, name="wb")
+            for gp in range(2):
+                for jj in range(2):
+                    nc.scalar.copy(
+                        out=wb[:, jj, 1024 * gp : 1024 * (gp + 1)],
+                        in_=wbys[k][:, jj, 1024 * gp : 1024 * (gp + 1)].bitcast(FP8),
+                    )
+            wbs[k] = wb
+
+        def transposes(halves, between=None):
+            banks = []
+            for g in range(PASSES):
+                words = halves[g // 2]
+                w0 = 256 * (g % 2)
+                tp = tpp.tile([P, 2, 256], F32, name="tp")
+                for u in range(2):
+                    for jj in range(2):
+                        nc.tensor.transpose(
+                            tp[:, u, jj * P : (jj + 1) * P],
+                            words[:, jj, w0 + u : w0 + 256 : 2],
+                            ident[:],
+                        )
+                banks.append(tp)
+                if between is not None:
+                    between(g)
+            return banks
+
+        def x_halves(b):
+            return [x_sb[(b, 0)][:].bitcast(F32), x_sb[(b, 1)][:].bitcast(F32)]
+
+        def w_halves(k):
+            wbw = wbs[k][:].bitcast(F32)
+            return [wbw[:, :, 0:512], wbw[:, :, 512:1024]]
+
+        def x_out(b, banks):
+            for g in range(PASSES):
+                dst_words = (
+                    xg[:, g, 256 * b : 256 * (b + 1), :]
+                    .rearrange("p r t -> p (r t)")
+                    .bitcast(F32)
+                    .rearrange("p (r u) -> p r u", u=2)
+                )
+                if b == 0:
+                    nc.vector.tensor_copy(out=dst_words, in_=banks[g][:].rearrange("p u r -> p r u"))
+                else:
+                    nc.scalar.copy(out=dst_words, in_=banks[g][:].rearrange("p u r -> p r u"))
+
+        def x_quant(gp):
+            nc.vector.quantize_mx(
+                out=xc[:, 2 * gp : 2 * gp + 2, :].rearrange("p g n -> p (g n)").bitcast(FP8X4),
+                scales=xs[:, 2 * gp : 2 * gp + 2, :].rearrange("p g n -> p (g n)"),
+                in_=xg[:, 2 * gp : 2 * gp + 2].rearrange("p g n t -> p (g n t)"),
+            )
+
+        def w_out(k, banks):
+            wg = wgp.tile([P, PASSES, 256, 4], BF16, name="wg", align_bytes=64)
+            for g in range(PASSES):
+                nc.vector.tensor_tensor(
+                    out=wg[:, g].rearrange("p r (u e) -> p r u e", u=2),
+                    in0=banks[g][:].bitcast(BF16).rearrange("p u (r e) -> p r u e", e=2),
+                    in1=sc4[:, g, :].rearrange("p (u e) -> p u e", u=2).unsqueeze(1).to_broadcast([P, 256, 2, 2]),
+                    op=ALU.mult,
+                )
+            wgs[k] = wg
+
+        def w_quant(k):
+            wc = wcp.tile([P, PASSES, 256], U32, name="wc", align_bytes=64)
+            ws = wcp.tile([P, PASSES, 256], U8, name="ws", align_bytes=64)
+            nc.vector.quantize_mx(
+                out=wc[:].rearrange("p g n -> p (g n)").bitcast(FP8X4),
+                scales=ws[:].rearrange("p g n -> p (g n)"),
+                in_=wgs[k][:].rearrange("p g n t -> p (g n t)"),
+            )
+            codes[k] = (wc, ws)
+
+        def products(k, jj):
+            wc, ws = codes[k]
+            acc = accp.tile([P, 512], F32, name="acc")
+            for g in range(PASSES):
+                nc.tensor.matmul_mx(
+                    out=acc[:],
+                    lhsT=wc[:, g, jj * P : (jj + 1) * P].bitcast(FP8X4),
+                    lhsT_scale=ws[:, g, jj * P : (jj + 1) * P],
+                    rhs=xc[:, g, :].bitcast(FP8X4),
+                    rhs_scale=xs[:, g, :],
+                    start=(g == 0),
+                    stop=(g == PASSES - 1),
+                )
+            accs[(k, jj)] = acc
+
+        def table(cs):
+            return tabs[:, cs, :].unsqueeze(1).to_broadcast([P, 2, 256])
+
+        def rotate_vector(k, jj):
+            if (k, jj) in ON_GPSIMD:
+                return
+            bias = biasc[:, 2 * k + jj : 2 * k + jj + 1]
+            pair = []
+            for cs in range(2):
+                t = uvp.tile([P, 512], F32, name="uv%d" % cs)
+                nc.vector.scalar_tensor_tensor(
+                    out=t[:].rearrange("p (b t) -> p b t", b=2),
+                    in0=accs[(k, jj)][:].rearrange("p (b t) -> p b t", b=2),
+                    scalar=bias,
+                    in1=table(cs),
+                    op0=ALU.add,
+                    op1=ALU.mult,
+                )
+                pair.append(t)
+            uvs[(k, jj)] = pair
+
+        def rotate_gpsimd(k, jj):
+            if (k, jj) not in ON_GPSIMD:
+                return
+            yt = ytp.tile([P, 512], F32, name="yt")
+            nc.scalar.activation(
+                out=yt[:], in_=accs[(k, jj)][:], func=ACT.Identity, bias=biasc[:, 2 * k + jj : 2 * k + jj + 1]
+            )
+            pair = []
+            for cs in range(2):
+                t = uvp.tile([P, 512], F32, name="uv%d" % cs)
+                nc.gpsimd.tensor_tensor(
+                    out=t[:].rearrange("p (b t) -> p b t", b=2),
+                    in0=yt[:].rearrange("p (b t) -> p b t", b=2),
+                    in1=table(cs),
+                    op=ALU.mult,
+                )
+                pair.append(t)
+            uvs[(k, jj)] = pair
+
+        def way_back(k, jj, b):
+            u, v = uvs[(k, jj)]
+            if b == 0:
+                backs[(k, jj)] = backp.tile([P, 4, P], F32, name="back")
+            back = backs[(k, jj)]
+            for tt in (2 * b, 2 * b + 1):
+                cols = slice(tt * P, (tt + 1) * P)
+                nc.tensor.matmul(out=back[:, tt, :], lhsT=u[:, cols], rhs=ident[:], start=True, stop=False, is_transpose=True)
+                nc.tensor.matmul(out=back[:, tt, :], lhsT=v[:, cols], rhs=perm[:], start=False, stop=True, is_transpose=True)
+
+        def leave(k, jj):
+            if k not in outs:
+                outs[k] = outp.tile([P, 2, 2, 2, P], F32, name="o")
+            o = outs[k]
+            if jj == 0:
+                nc.scalar.copy(out=o[:, :, jj, :, :], in_=backs[(k, jj)][:].rearrange("p (b e) d -> p b e d", b=2))
+            else:
+                nc.vector.tensor_copy(out=o[:, :, jj, :, :], in_=backs[(k, jj)][:].rearrange("p (b e) d -> p b e d", b=2))
+            if jj == 0:
+                dst = out_0 if k < 8 else out_1
+                h0 = 2 * (k % 8)
+                for b in range(2):
+                    nc.sync.dma_start(
+                        out=dst[b, h0 : h0 + 2].rearrange("h (p e) d -> p h (e d)", e=2),
+                        in_=o[:, b].rearrange("p h e d -> p h (e d)"),
+                    )
+
+        with tc.manual_schedule():
+            load_w(0)
+            load_x(0, 0)
+            nc.sync.dma_start(out=sc4[:], in_=Wqk_scale.rearrange("o (g p t) -> p (o g) t", p=P, t=4))
+            load_x(0, 1)
+            load_w(1)
+            load_x(1, 0)
+            load_x(1, 1)
+            nc.sync.dma_start(out=cos_sb[:], in_=cos.rearrange("(p e) i -> p e i", e=2))
+            nc.sync.dma_start(out=sin_sb[:], in_=sin.rearrange("(p e) i -> p e i", e=2))
+            nc.sync.dma_start(out=brow_bf[:], in_=bqk.rearrange("(j p) -> j p", p=P))
+            for k in range(2, NSTEP):
+                load_w(k)
+
+            nc.gpsimd.tensor_copy(out=perm[:, 0:64], in_=ident[:, 64:128])
+            nc.gpsimd.tensor_copy(out=perm[:, 64:128], in_=ident[:, 0:64])
+            nc.gpsimd.memset(brow[:], 0.0)
+            nc.gpsimd.tensor_copy(out=nat[:, 0], in_=cos_sb[:].unsqueeze(2).to_broadcast([P, 2, 2, 64]))
+            nc.gpsimd.tensor_copy(out=nat[:, 1, :, 0, :], in_=sin_sb[:])
+            nc.gpsimd.tensor_scalar(out=nat[:, 1, :, 1, :], in0=sin_sb[:], scalar1=-1.0, scalar2=0.0, op0=ALU.mult, op1=ALU.add)
+            nc.gpsimd.tensor_copy(out=brow[0:32, :], in_=brow_bf[:])
+
+            casts(0)
+            casts(1)
+            x_out(0, transposes(x_halves(0)))
+            w_out(0, transposes(w_halves(0)))
+            x_out(1, transposes(x_halves(1)))
+            casts(2)
+            tb = tpp.tile([P, 2, 256], F32, name="tp")
+            tbv = tb[:].rearrange("p a (b c) -> p (a b) c", b=2)
+            natv = nat[:].rearrange("p s e a i -> p (s e) (a i)")
+            for q in range(4):
+                nc.tensor.transpose(tbv[:, q, :], natv[:, q, :], ident[:])
+            bb = tpp.tile([P, 2, 256], F32, name="tp")
+            nc.tensor.transpose(bb[:, 0, 0:P], brow[:], ident[:])
+            nc.vector.tensor_copy(out=tabs[:].rearrange("p s t -> p (s t)"), in_=tb[:].rearrange("p a c -> p (a c)"))
+            nc.vector.tensor_copy(out=biasc[:], in_=bb[:, 0, 0:32])
+            x_quant(0)
+            x_quant(1)
+            w_quant(0)
+
+            for i in range(NSTEP + 2):
+                if i >= 1 and i + 2 < NSTEP:
+                    casts(i + 2)
+                if i + 1 < NSTEP and 2 <= i:
+                    banks = transposes(w_halves(i + 1), lambda g: way_back(i - 2, g // 2, g % 2))
+                elif i + 1 < NSTEP:
+                    banks = transposes(w_halves(i + 1))
+                else:
+                    for g in range(PASSES):
+                        way_back(i - 2, g // 2, g % 2)
+                if i < NSTEP:
+                    products(i, 0)
+                    products(i, 1)
+                if i + 1 < NSTEP:
+                    w_out(i + 1, banks)
+                if 2 <= i:
+                    leave(i - 2, 1)
+                if i + 1 < NSTEP:
+                    w_quant(i + 1)
+                if i < NSTEP:
+                    rotate_vector(i, 0)
+                    rotate_vector(i, 1)
+                if 2 <= i:
+                    leave(i - 2, 0)
+                if i < NSTEP:
+                    rotate_gpsimd(i, 0)
+                    rotate_gpsimd(i, 1)

@@ -76,22 +76,23 @@ def tile_selfattention_pa_kernel(tc, x, Wqk_bytes, Wqk_scale, bqk, cos, sin, out
 
         make_identity(nc, ident[:])
 
-        def casts(k):
-            wb = wbp.tile([P, 2, K], BF16, name="wb")
-            for gp in range(2):
+        def casts(k, halves=(0, 1)):
+            if k not in wbs:
+                wbs[k] = wbp.tile([P, 2, K], BF16, name="wb")
+            wb = wbs[k]
+            for gp in halves:
                 for jj in range(2):
                     nc.scalar.copy(
                         out=wb[:, jj, 1024 * gp : 1024 * (gp + 1)],
                         in_=wbys[k][:, jj, 1024 * gp : 1024 * (gp + 1)].bitcast(FP8),
                     )
-            wbs[k] = wb
 
-        def transposes(halves, between=None):
+        def transposes(halves, between=None, spare=None):
             banks = []
             for g in range(PASSES):
                 words = halves[g // 2]
                 w0 = 256 * (g % 2)
-                tp = tpp.tile([P, 2, 256], F32, name="tp")
+                tp = spare[g] if spare is not None else tpp.tile([P, 2, 256], F32, name="tp")[:]
                 for u in range(2):
                     for jj in range(2):
                         nc.tensor.transpose(
@@ -120,9 +121,9 @@ def tile_selfattention_pa_kernel(tc, x, Wqk_bytes, Wqk_scale, bqk, cos, sin, out
                     .rearrange("p (r u) -> p r u", u=2)
                 )
                 if b == 0:
-                    nc.vector.tensor_copy(out=dst_words, in_=banks[g][:].rearrange("p u r -> p r u"))
+                    nc.vector.tensor_copy(out=dst_words, in_=banks[g].rearrange("p u r -> p r u"))
                 else:
-                    nc.scalar.copy(out=dst_words, in_=banks[g][:].rearrange("p u r -> p r u"))
+                    nc.scalar.copy(out=dst_words, in_=banks[g].rearrange("p u r -> p r u"))
 
         def x_quant(gp):
             nc.vector.quantize_mx(
@@ -136,7 +137,7 @@ def tile_selfattention_pa_kernel(tc, x, Wqk_bytes, Wqk_scale, bqk, cos, sin, out
             for g in range(PASSES):
                 nc.vector.tensor_tensor(
                     out=wg[:, g].rearrange("p r (u e) -> p r u e", u=2),
-                    in0=banks[g][:].bitcast(BF16).rearrange("p u (r e) -> p r u e", e=2),
+                    in0=banks[g].bitcast(BF16).rearrange("p u (r e) -> p r u e", e=2),
                     in1=sc4[:, g, :].rearrange("p (u e) -> p u e", u=2).unsqueeze(1).to_broadcast([P, 256, 2, 2]),
                     op=ALU.mult,
                 )
@@ -209,8 +210,10 @@ def tile_selfattention_pa_kernel(tc, x, Wqk_bytes, Wqk_scale, bqk, cos, sin, out
 
         def way_back(k, jj, b):
             u, v = uvs[(k, jj)]
-            if b == 0:
-                backs[(k, jj)] = backp.tile([P, 4, P], F32, name="back")
+            if b == 0 and k >= NSTEP - 2:
+                backs[(k, jj)] = tpp.tile([P, 2, 256], F32, name="tp")[:].rearrange("p a (c d) -> p (a c) d", c=2)
+            elif b == 0:
+                backs[(k, jj)] = backp.tile([P, 4, P], F32, name="back")[:]
             back = backs[(k, jj)]
             for tt in (2 * b, 2 * b + 1):
                 cols = slice(tt * P, (tt + 1) * P)
@@ -222,9 +225,9 @@ def tile_selfattention_pa_kernel(tc, x, Wqk_bytes, Wqk_scale, bqk, cos, sin, out
                 outs[k] = outp.tile([P, 2, 2, 2, P], F32, name="o")
             o = outs[k]
             if jj == 0:
-                nc.scalar.copy(out=o[:, :, jj, :, :], in_=backs[(k, jj)][:].rearrange("p (b e) d -> p b e d", b=2))
+                nc.scalar.copy(out=o[:, :, jj, :, :], in_=backs[(k, jj)].rearrange("p (b e) d -> p b e d", b=2))
             else:
-                nc.vector.tensor_copy(out=o[:, :, jj, :, :], in_=backs[(k, jj)][:].rearrange("p (b e) d -> p b e d", b=2))
+                nc.vector.tensor_copy(out=o[:, :, jj, :, :], in_=backs[(k, jj)].rearrange("p (b e) d -> p b e d", b=2))
             if jj == 0:
                 dst = out_0 if k < 8 else out_1
                 h0 = 2 * (k % 8)
@@ -257,11 +260,14 @@ def tile_selfattention_pa_kernel(tc, x, Wqk_bytes, Wqk_scale, bqk, cos, sin, out
             nc.gpsimd.tensor_copy(out=brow[0:32, :], in_=brow_bf[:])
 
             casts(0)
-            casts(1)
+            casts(1, (0,))
             x_out(0, transposes(x_halves(0)))
-            w_out(0, transposes(w_halves(0)))
-            x_out(1, transposes(x_halves(1)))
-            casts(2)
+            w0_banks = transposes(w_halves(0))
+            spare = [accp.tile([P, 512], F32, name="acc")[:].rearrange("p (u r) -> p u r", u=2) for g in range(2)]
+            spare += [backp.tile([P, 4, P], F32, name="back")[:].rearrange("p (u c) d -> p u (c d)", u=2) for g in range(2)]
+            x_out(1, transposes(x_halves(1), spare=spare))
+            w_out(0, w0_banks)
+            casts(1, (1,))
             tb = tpp.tile([P, 2, 256], F32, name="tp")
             tbv = tb[:].rearrange("p a (b c) -> p (a b) c", b=2)
             natv = nat[:].rearrange("p s e a i -> p (s e) (a i)")
@@ -269,11 +275,12 @@ def tile_selfattention_pa_kernel(tc, x, Wqk_bytes, Wqk_scale, bqk, cos, sin, out
                 nc.tensor.transpose(tbv[:, q, :], natv[:, q, :], ident[:])
             bb = tpp.tile([P, 2, 256], F32, name="tp")
             nc.tensor.transpose(bb[:, 0, 0:P], brow[:], ident[:])
-            nc.vector.tensor_copy(out=tabs[:].rearrange("p s t -> p (s t)"), in_=tb[:].rearrange("p a c -> p (a c)"))
-            nc.vector.tensor_copy(out=biasc[:], in_=bb[:, 0, 0:32])
+            w_quant(0)
+            nc.scalar.copy(out=biasc[:], in_=bb[:, 0, 0:32])
+            nc.scalar.copy(out=tabs[:].rearrange("p s t -> p (s t)"), in_=tb[:].rearrange("p a c -> p (a c)"))
+            casts(2)
             x_quant(0)
             x_quant(1)
-            w_quant(0)
 
             for i in range(NSTEP + 2):
                 if i >= 1 and i + 2 < NSTEP:
@@ -282,6 +289,14 @@ def tile_selfattention_pa_kernel(tc, x, Wqk_bytes, Wqk_scale, bqk, cos, sin, out
                     banks = transposes(w_halves(i + 1), lambda g: way_back(i - 2, g // 2, g % 2))
                 elif i + 1 < NSTEP:
                     banks = transposes(w_halves(i + 1))
+                elif i == NSTEP - 1:
+                    for g in range(PASSES):
+                        way_back(i - 2, g // 2, g % 2)
+                    way_back(i - 1, 0, 0)
+                    way_back(i - 1, 0, 1)
+                elif i == NSTEP:
+                    way_back(i - 2, 1, 0)
+                    way_back(i - 2, 1, 1)
                 else:
                     for g in range(PASSES):
                         way_back(i - 2, g // 2, g % 2)

@@ -87,9 +87,9 @@ def tile_selfattention_pa_kernel(tc, x, Wqk_bytes, Wqk_scale, bqk, cos, sin, out
                         in_=wbys[k][:, jj, 1024 * gp : 1024 * (gp + 1)].bitcast(FP8),
                     )
 
-        def transposes(halves, between=None, spare=None):
+        def transposes(halves, between=None, spare=None, passes=range(PASSES)):
             banks = []
-            for g in range(PASSES):
+            for g in passes:
                 words = halves[g // 2]
                 w0 = 256 * (g % 2)
                 tp = spare[g] if spare is not None else tpp.tile([P, 2, 256], F32, name="tp")[:]
@@ -120,10 +120,7 @@ def tile_selfattention_pa_kernel(tc, x, Wqk_bytes, Wqk_scale, bqk, cos, sin, out
                     .bitcast(F32)
                     .rearrange("p (r u) -> p r u", u=2)
                 )
-                if b == 0:
-                    nc.vector.tensor_copy(out=dst_words, in_=banks[g].rearrange("p u r -> p r u"))
-                else:
-                    nc.scalar.copy(out=dst_words, in_=banks[g].rearrange("p u r -> p r u"))
+                nc.scalar.copy(out=dst_words, in_=banks[g].rearrange("p u r -> p r u"))
 
         def x_quant(gp):
             nc.vector.quantize_mx(
@@ -260,12 +257,15 @@ def tile_selfattention_pa_kernel(tc, x, Wqk_bytes, Wqk_scale, bqk, cos, sin, out
             nc.gpsimd.tensor_copy(out=brow[0:32, :], in_=brow_bf[:])
 
             casts(0)
-            casts(1, (0,))
-            x_out(0, transposes(x_halves(0)))
-            w0_banks = transposes(w_halves(0))
             spare = [accp.tile([P, 512], F32, name="acc")[:].rearrange("p (u r) -> p u r", u=2) for g in range(2)]
             spare += [backp.tile([P, 4, P], F32, name="back")[:].rearrange("p (u c) d -> p u (c d)", u=2) for g in range(2)]
-            x_out(1, transposes(x_halves(1), spare=spare))
+            x0_banks = transposes(x_halves(0), passes=(0, 1))
+            w0_banks = transposes(w_halves(0), spare=spare, passes=(0, 1))
+            x0_banks += transposes(x_halves(0), passes=(2, 3))
+            w0_banks += transposes(w_halves(0), spare=spare, passes=(2, 3))
+            x_out(0, x0_banks)
+            casts(1, (0,))
+            x_out(1, transposes(x_halves(1)))
             w_out(0, w0_banks)
             casts(1, (1,))
             tb = tpp.tile([P, 2, 256], F32, name="tp")

@@ -18,6 +18,7 @@ PASSES = 4
 NSTEP = 16
 FLOPS = 2 * 512 * 4096 * 2048
 
+BOTH_ON_SCALAR = (6, 12)
 ON_GPSIMD = tuple((k, jj) for k in range(NSTEP - 1) for jj in range(2))
 
 
@@ -80,6 +81,10 @@ def tile_selfattention_pa_kernel(tc, x, Wqk_bytes, Wqk_scale, bqk, cos, sin, out
             if k not in wbs:
                 wbs[k] = wbp.tile([P, 2, K], BF16, name="wb")
             wb = wbs[k]
+            if 3 <= k < NSTEP - 2:
+                for jj in range(2):
+                    nc.scalar.copy(out=wb[:, jj, :], in_=wbys[k][:, jj, :].bitcast(FP8))
+                return
             for gp in halves:
                 for jj in range(2):
                     nc.scalar.copy(
@@ -120,7 +125,10 @@ def tile_selfattention_pa_kernel(tc, x, Wqk_bytes, Wqk_scale, bqk, cos, sin, out
                     .bitcast(F32)
                     .rearrange("p (r u) -> p r u", u=2)
                 )
-                nc.scalar.copy(out=dst_words, in_=banks[g].rearrange("p u r -> p r u"))
+                if b == 0 and g < 2:
+                    nc.vector.tensor_copy(out=dst_words, in_=banks[g].rearrange("p u r -> p r u"))
+                else:
+                    nc.scalar.copy(out=dst_words, in_=banks[g].rearrange("p u r -> p r u"))
 
         def x_quant(gp):
             nc.vector.quantize_mx(
@@ -221,7 +229,7 @@ def tile_selfattention_pa_kernel(tc, x, Wqk_bytes, Wqk_scale, bqk, cos, sin, out
             if k not in outs:
                 outs[k] = outp.tile([P, 2, 2, 2, P], F32, name="o")
             o = outs[k]
-            if jj == 0:
+            if jj == 0 or k in BOTH_ON_SCALAR:
                 nc.scalar.copy(out=o[:, :, jj, :, :], in_=backs[(k, jj)].rearrange("p (b e) d -> p b e d", b=2))
             else:
                 nc.vector.tensor_copy(out=o[:, :, jj, :, :], in_=backs[(k, jj)].rearrange("p (b e) d -> p b e d", b=2))

@@ -15,24 +15,24 @@ ACT = mybir.ActivationFunctionType
 P = 128
 K = 2048
 PASSES = 4
-NSTEP = 16
+HEADS = 32
 FLOPS = 2 * 512 * 4096 * 2048
 
-BOTH_ON_SCALAR = (6, 12)
-ON_GPSIMD = tuple((k, jj) for k in range(NSTEP - 1) for jj in range(2))
+ROT_ON_VECTOR = (30, 31)
+CAST_ON_VECTOR = (0,)
 
 
 def tile_selfattention_pa_kernel(tc, x, Wqk_bytes, Wqk_scale, bqk, cos, sin, out_0, out_1):
     nc = tc.nc
     with ExitStack() as ctx:
         const = ctx.enter_context(tc.tile_pool(name="const", bufs=1))
-        wraw = ctx.enter_context(tc.tile_pool(name="wraw", bufs=NSTEP))
-        wbp = ctx.enter_context(tc.tile_pool(name="wbp", bufs=3))
-        wgp = ctx.enter_context(tc.tile_pool(name="wgp", bufs=2))
-        wcp = ctx.enter_context(tc.tile_pool(name="wcp", bufs=2))
-        uvp = ctx.enter_context(tc.tile_pool(name="uvp", bufs=6))
+        wraw = ctx.enter_context(tc.tile_pool(name="wraw", bufs=HEADS))
+        wbp = ctx.enter_context(tc.tile_pool(name="wbp", bufs=5))
+        wgp = ctx.enter_context(tc.tile_pool(name="wgp", bufs=3))
+        wcp = ctx.enter_context(tc.tile_pool(name="wcp", bufs=3))
+        uvp = ctx.enter_context(tc.tile_pool(name="uvp", bufs=5))
         ytp = ctx.enter_context(tc.tile_pool(name="ytp", bufs=3))
-        outp = ctx.enter_context(tc.tile_pool(name="outp", bufs=4))
+        outp = ctx.enter_context(tc.tile_pool(name="outp", bufs=6))
         tpp = ctx.enter_context(tc.psum_pool(name="tpp", bufs=4))
         accp = ctx.enter_context(tc.psum_pool(name="accp", bufs=2))
         backp = ctx.enter_context(tc.psum_pool(name="backp", bufs=2))
@@ -44,7 +44,7 @@ def tile_selfattention_pa_kernel(tc, x, Wqk_bytes, Wqk_scale, bqk, cos, sin, out
         accs = {}
         uvs = {}
         backs = {}
-        outs = {}
+        w_banks = {}
 
         x_sb = {}
         for b in range(2):
@@ -70,192 +70,22 @@ def tile_selfattention_pa_kernel(tc, x, Wqk_bytes, Wqk_scale, bqk, cos, sin, out
                 in_=x[b].rearrange("(p e) k -> p e k", e=2)[:, :, 1024 * half : 1024 * (half + 1)],
             )
 
-        def load_w(k):
-            wby = wraw.tile([P, 2, K], U8, name="wby")
-            nc.sync.dma_start(out=wby[:], in_=Wqk_bytes[256 * k : 256 * (k + 1), :].rearrange("(j p) k -> p j k", p=P))
-            wbys[k] = wby
+        def load_w(n):
+            wby = wraw.tile([P, K], U8, name="wby")
+            nc.sync.dma_start(out=wby[:], in_=Wqk_bytes[P * n : P * (n + 1), :])
+            wbys[n] = wby
 
         make_identity(nc, ident[:])
 
-        def casts(k, halves=(0, 1)):
-            if k not in wbs:
-                wbs[k] = wbp.tile([P, 2, K], BF16, name="wb")
-            wb = wbs[k]
-            if 3 <= k < NSTEP - 2:
-                for jj in range(2):
-                    nc.scalar.copy(out=wb[:, jj, :], in_=wbys[k][:, jj, :].bitcast(FP8))
-                return
-            for gp in halves:
-                for jj in range(2):
-                    nc.scalar.copy(
-                        out=wb[:, jj, 1024 * gp : 1024 * (gp + 1)],
-                        in_=wbys[k][:, jj, 1024 * gp : 1024 * (gp + 1)].bitcast(FP8),
-                    )
-
-        def transposes(halves, between=None, spare=None, passes=range(PASSES)):
-            banks = []
-            for g in passes:
-                words = halves[g // 2]
-                w0 = 256 * (g % 2)
-                tp = spare[g] if spare is not None else tpp.tile([P, 2, 256], F32, name="tp")[:]
-                for u in range(2):
-                    for jj in range(2):
-                        nc.tensor.transpose(
-                            tp[:, u, jj * P : (jj + 1) * P],
-                            words[:, jj, w0 + u : w0 + 256 : 2],
-                            ident[:],
-                        )
-                banks.append(tp)
-                if between is not None:
-                    between(g)
-            return banks
-
-        def x_halves(b):
-            return [x_sb[(b, 0)][:].bitcast(F32), x_sb[(b, 1)][:].bitcast(F32)]
-
-        def w_halves(k):
-            wbw = wbs[k][:].bitcast(F32)
-            return [wbw[:, :, 0:512], wbw[:, :, 512:1024]]
-
-        def x_out(b, banks):
-            for g in range(PASSES):
-                dst_words = (
-                    xg[:, g, 256 * b : 256 * (b + 1), :]
-                    .rearrange("p r t -> p (r t)")
-                    .bitcast(F32)
-                    .rearrange("p (r u) -> p r u", u=2)
-                )
-                if b == 0 and g < 2:
-                    nc.vector.tensor_copy(out=dst_words, in_=banks[g].rearrange("p u r -> p r u"))
-                else:
-                    nc.scalar.copy(out=dst_words, in_=banks[g].rearrange("p u r -> p r u"))
-
-        def x_quant(gp):
-            nc.vector.quantize_mx(
-                out=xc[:, 2 * gp : 2 * gp + 2, :].rearrange("p g n -> p (g n)").bitcast(FP8X4),
-                scales=xs[:, 2 * gp : 2 * gp + 2, :].rearrange("p g n -> p (g n)"),
-                in_=xg[:, 2 * gp : 2 * gp + 2].rearrange("p g n t -> p (g n t)"),
-            )
-
-        def w_out(k, banks):
-            wg = wgp.tile([P, PASSES, 256, 4], BF16, name="wg", align_bytes=64)
-            for g in range(PASSES):
-                nc.vector.tensor_tensor(
-                    out=wg[:, g].rearrange("p r (u e) -> p r u e", u=2),
-                    in0=banks[g].bitcast(BF16).rearrange("p u (r e) -> p r u e", e=2),
-                    in1=sc4[:, g, :].rearrange("p (u e) -> p u e", u=2).unsqueeze(1).to_broadcast([P, 256, 2, 2]),
-                    op=ALU.mult,
-                )
-            wgs[k] = wg
-
-        def w_quant(k):
-            wc = wcp.tile([P, PASSES, 256], U32, name="wc", align_bytes=64)
-            ws = wcp.tile([P, PASSES, 256], U8, name="ws", align_bytes=64)
-            nc.vector.quantize_mx(
-                out=wc[:].rearrange("p g n -> p (g n)").bitcast(FP8X4),
-                scales=ws[:].rearrange("p g n -> p (g n)"),
-                in_=wgs[k][:].rearrange("p g n t -> p (g n t)"),
-            )
-            codes[k] = (wc, ws)
-
-        def products(k, jj):
-            wc, ws = codes[k]
-            acc = accp.tile([P, 512], F32, name="acc")
-            for g in range(PASSES):
-                nc.tensor.matmul_mx(
-                    out=acc[:],
-                    lhsT=wc[:, g, jj * P : (jj + 1) * P].bitcast(FP8X4),
-                    lhsT_scale=ws[:, g, jj * P : (jj + 1) * P],
-                    rhs=xc[:, g, :].bitcast(FP8X4),
-                    rhs_scale=xs[:, g, :],
-                    start=(g == 0),
-                    stop=(g == PASSES - 1),
-                )
-            accs[(k, jj)] = acc
-
-        def table(cs):
-            return tabs[:, cs, :].unsqueeze(1).to_broadcast([P, 2, 256])
-
-        def rotate_vector(k, jj):
-            if (k, jj) in ON_GPSIMD:
-                return
-            bias = biasc[:, 2 * k + jj : 2 * k + jj + 1]
-            pair = []
-            for cs in range(2):
-                t = uvp.tile([P, 512], F32, name="uv%d" % cs)
-                nc.vector.scalar_tensor_tensor(
-                    out=t[:].rearrange("p (b t) -> p b t", b=2),
-                    in0=accs[(k, jj)][:].rearrange("p (b t) -> p b t", b=2),
-                    scalar=bias,
-                    in1=table(cs),
-                    op0=ALU.add,
-                    op1=ALU.mult,
-                )
-                pair.append(t)
-            uvs[(k, jj)] = pair
-
-        def rotate_gpsimd(k, jj):
-            if (k, jj) not in ON_GPSIMD:
-                return
-            yt = ytp.tile([P, 512], F32, name="yt")
-            nc.scalar.activation(
-                out=yt[:], in_=accs[(k, jj)][:], func=ACT.Identity, bias=biasc[:, 2 * k + jj : 2 * k + jj + 1]
-            )
-            pair = []
-            for cs in range(2):
-                t = uvp.tile([P, 512], F32, name="uv%d" % cs)
-                nc.gpsimd.tensor_tensor(
-                    out=t[:].rearrange("p (b t) -> p b t", b=2),
-                    in0=yt[:].rearrange("p (b t) -> p b t", b=2),
-                    in1=table(cs),
-                    op=ALU.mult,
-                )
-                pair.append(t)
-            uvs[(k, jj)] = pair
-
-        def way_back(k, jj, b):
-            u, v = uvs[(k, jj)]
-            if b == 0 and k >= NSTEP - 2:
-                backs[(k, jj)] = tpp.tile([P, 2, 256], F32, name="tp")[:].rearrange("p a (c d) -> p (a c) d", c=2)
-            elif b == 0:
-                backs[(k, jj)] = backp.tile([P, 4, P], F32, name="back")[:]
-            back = backs[(k, jj)]
-            for tt in (2 * b, 2 * b + 1):
-                cols = slice(tt * P, (tt + 1) * P)
-                nc.tensor.matmul(out=back[:, tt, :], lhsT=u[:, cols], rhs=ident[:], start=True, stop=False, is_transpose=True)
-                nc.tensor.matmul(out=back[:, tt, :], lhsT=v[:, cols], rhs=perm[:], start=False, stop=True, is_transpose=True)
-
-        def leave(k, jj):
-            if k not in outs:
-                outs[k] = outp.tile([P, 2, 2, 2, P], F32, name="o")
-            o = outs[k]
-            if jj == 0 or k in BOTH_ON_SCALAR:
-                nc.scalar.copy(out=o[:, :, jj, :, :], in_=backs[(k, jj)].rearrange("p (b e) d -> p b e d", b=2))
-            else:
-                nc.vector.tensor_copy(out=o[:, :, jj, :, :], in_=backs[(k, jj)].rearrange("p (b e) d -> p b e d", b=2))
-            if jj == 0:
-                dst = out_0 if k < 8 else out_1
-                h0 = 2 * (k % 8)
-                for b in range(2):
-                    nc.sync.dma_start(
-                        out=dst[b, h0 : h0 + 2].rearrange("h (p e) d -> p h (e d)", e=2),
-                        in_=o[:, b].rearrange("p h e d -> p h (e d)"),
-                    )
-
-        with tc.manual_schedule():
-            load_w(0)
-            load_x(0, 0)
+        def load_scales():
             nc.sync.dma_start(out=sc4[:], in_=Wqk_scale.rearrange("o (g p t) -> p (o g) t", p=P, t=4))
-            load_x(0, 1)
-            load_w(1)
-            load_x(1, 0)
-            load_x(1, 1)
+
+        def load_tables():
             nc.sync.dma_start(out=cos_sb[:], in_=cos.rearrange("(p e) i -> p e i", e=2))
             nc.sync.dma_start(out=sin_sb[:], in_=sin.rearrange("(p e) i -> p e i", e=2))
             nc.sync.dma_start(out=brow_bf[:], in_=bqk.rearrange("(j p) -> j p", p=P))
-            for k in range(2, NSTEP):
-                load_w(k)
 
+        def constants():
             nc.gpsimd.tensor_copy(out=perm[:, 0:64], in_=ident[:, 64:128])
             nc.gpsimd.tensor_copy(out=perm[:, 64:128], in_=ident[:, 0:64])
             nc.gpsimd.memset(brow[:], 0.0)
@@ -264,18 +94,7 @@ def tile_selfattention_pa_kernel(tc, x, Wqk_bytes, Wqk_scale, bqk, cos, sin, out
             nc.gpsimd.tensor_scalar(out=nat[:, 1, :, 1, :], in0=sin_sb[:], scalar1=-1.0, scalar2=0.0, op0=ALU.mult, op1=ALU.add)
             nc.gpsimd.tensor_copy(out=brow[0:32, :], in_=brow_bf[:])
 
-            casts(0)
-            spare = [accp.tile([P, 512], F32, name="acc")[:].rearrange("p (u r) -> p u r", u=2) for g in range(2)]
-            spare += [backp.tile([P, 4, P], F32, name="back")[:].rearrange("p (u c) d -> p u (c d)", u=2) for g in range(2)]
-            x0_banks = transposes(x_halves(0), passes=(0, 1))
-            w0_banks = transposes(w_halves(0), spare=spare, passes=(0, 1))
-            x0_banks += transposes(x_halves(0), passes=(2, 3))
-            w0_banks += transposes(w_halves(0), spare=spare, passes=(2, 3))
-            x_out(0, x0_banks)
-            casts(1, (0,))
-            x_out(1, transposes(x_halves(1)))
-            w_out(0, w0_banks)
-            casts(1, (1,))
+        def tables():
             tb = tpp.tile([P, 2, 256], F32, name="tp")
             tbv = tb[:].rearrange("p a (b c) -> p (a b) c", b=2)
             natv = nat[:].rearrange("p s e a i -> p (s e) (a i)")
@@ -283,45 +102,218 @@ def tile_selfattention_pa_kernel(tc, x, Wqk_bytes, Wqk_scale, bqk, cos, sin, out
                 nc.tensor.transpose(tbv[:, q, :], natv[:, q, :], ident[:])
             bb = tpp.tile([P, 2, 256], F32, name="tp")
             nc.tensor.transpose(bb[:, 0, 0:P], brow[:], ident[:])
-            w_quant(0)
+            return tb, bb
+
+        def tables_out(banks):
+            tb, bb = banks
             nc.scalar.copy(out=biasc[:], in_=bb[:, 0, 0:32])
             nc.scalar.copy(out=tabs[:].rearrange("p s t -> p (s t)"), in_=tb[:].rearrange("p a c -> p (a c)"))
-            casts(2)
+
+        def cast(n, parts=1):
+            wb = wbp.tile([P, K], BF16, name="wb")
+            width = K // parts
+            for part in range(parts):
+                cols = slice(width * part, width * (part + 1))
+                if n in CAST_ON_VECTOR:
+                    nc.vector.tensor_copy(out=wb[:, cols], in_=wbys[n][:, cols].bitcast(FP8))
+                else:
+                    nc.scalar.copy(out=wb[:, cols], in_=wbys[n][:, cols].bitcast(FP8))
+            wbs[n] = wb
+
+        def new_bank(pool):
+            if pool == "tp":
+                return tpp.tile([P, 2, 256], F32, name="tp")[:]
+            if pool == "acc":
+                return accp.tile([P, 512], F32, name="acc")[:].rearrange("p (u r) -> p u r", u=2)
+            return backp.tile([P, 4, P], F32, name="back")[:].rearrange("p (u c) d -> p u (c d)", u=2)
+
+        def w_transposes(n, pool="tp"):
+            words = wbs[n][:].bitcast(F32)
+            w_banks[n] = []
+            for gp in range(2):
+                tp = new_bank(pool)
+                for u in range(2):
+                    for gg in range(2):
+                        w0 = 256 * (2 * gp + gg)
+                        nc.tensor.transpose(tp[:, u, gg * P : (gg + 1) * P], words[:, w0 + u : w0 + 256 : 2], ident[:])
+                w_banks[n].append(tp)
+
+        def x_transposes(b, g, pool="tp"):
+            words = x_sb[(b, g // 2)][:].bitcast(F32)
+            w0 = 256 * (g % 2)
+            tp = new_bank(pool)
+            for u in range(2):
+                for e in range(2):
+                    nc.tensor.transpose(tp[:, u, e * P : (e + 1) * P], words[:, e, w0 + u : w0 + 256 : 2], ident[:])
+            return tp
+
+        def x_out(b, g, bank, on_vector=False):
+            dst_words = (
+                xg[:, g, 256 * b : 256 * (b + 1), :]
+                .rearrange("p r t -> p (r t)")
+                .bitcast(F32)
+                .rearrange("p (r u) -> p r u", u=2)
+            )
+            src = bank.rearrange("p u r -> p r u")
+            if on_vector:
+                nc.vector.tensor_copy(out=dst_words, in_=src)
+            else:
+                nc.scalar.copy(out=dst_words, in_=src)
+
+        def x_quant(gp):
+            nc.vector.quantize_mx(
+                out=xc[:, 2 * gp : 2 * gp + 2, :].rearrange("p g n -> p (g n)").bitcast(FP8X4),
+                scales=xs[:, 2 * gp : 2 * gp + 2, :].rearrange("p g n -> p (g n)"),
+                in_=xg[:, 2 * gp : 2 * gp + 2].rearrange("p g n t -> p (g n t)"),
+            )
+
+        def w_out(n, gp):
+            if gp == 0:
+                wgs[n] = wgp.tile([P, PASSES, P, 4], BF16, name="wg", align_bytes=64)
+            nc.vector.tensor_tensor(
+                out=wgs[n][:, 2 * gp : 2 * gp + 2].rearrange("p g r (u e) -> p g r u e", u=2),
+                in0=w_banks[n][gp].bitcast(BF16).rearrange("p u (g r e) -> p g r u e", g=2, e=2),
+                in1=sc4[:, 2 * gp : 2 * gp + 2, :]
+                .rearrange("p g (u e) -> p g u e", u=2)
+                .unsqueeze(2)
+                .to_broadcast([P, 2, P, 2, 2]),
+                op=ALU.mult,
+            )
+
+        def w_quant(n):
+            wc = wcp.tile([P, PASSES, P], U32, name="wc", align_bytes=64)
+            ws = wcp.tile([P, PASSES, P], U8, name="ws", align_bytes=64)
+            nc.vector.quantize_mx(
+                out=wc[:].rearrange("p g n -> p (g n)").bitcast(FP8X4),
+                scales=ws[:].rearrange("p g n -> p (g n)"),
+                in_=wgs[n][:].rearrange("p g n t -> p (g n t)"),
+            )
+            codes[n] = (wc, ws)
+
+        def products(n):
+            wc, ws = codes[n]
+            acc = accp.tile([P, 512], F32, name="acc")
+            for g in range(PASSES):
+                nc.tensor.matmul_mx(
+                    out=acc[:],
+                    lhsT=wc[:, g, :].bitcast(FP8X4),
+                    lhsT_scale=ws[:, g, :],
+                    rhs=xc[:, g, :].bitcast(FP8X4),
+                    rhs_scale=xs[:, g, :],
+                    start=(g == 0),
+                    stop=(g == PASSES - 1),
+                )
+            accs[n] = acc
+
+        def table(cs):
+            return tabs[:, cs, :].unsqueeze(1).to_broadcast([P, 2, 256])
+
+        def rotate_vector(n):
+            uv = uvp.tile([P, 2, 512], F32, name="uv")
+            for cs in range(2):
+                nc.vector.scalar_tensor_tensor(
+                    out=uv[:, cs, :].rearrange("p (b t) -> p b t", b=2),
+                    in0=accs[n][:].rearrange("p (b t) -> p b t", b=2),
+                    scalar=biasc[:, n : n + 1],
+                    in1=table(cs),
+                    op0=ALU.add,
+                    op1=ALU.mult,
+                )
+            uvs[n] = uv
+
+        def add_bias(n):
+            yt = ytp.tile([P, 512], F32, name="yt")
+            nc.scalar.activation(out=yt[:], in_=accs[n][:], func=ACT.Identity, bias=biasc[:, n : n + 1])
+            uvs[n] = yt
+
+        def rotate_gpsimd(n):
+            uv = uvp.tile([P, 2, 512], F32, name="uv")
+            nc.gpsimd.tensor_tensor(
+                out=uv[:].rearrange("p s (b t) -> p s b t", b=2),
+                in0=uvs[n][:].rearrange("p (b t) -> p b t", b=2).unsqueeze(1).to_broadcast([P, 2, 2, 256]),
+                in1=tabs[:].unsqueeze(2).to_broadcast([P, 2, 2, 256]),
+                op=ALU.mult,
+            )
+            uvs[n] = uv
+
+        def way_back(n):
+            uv = uvs[n]
+            back = backp.tile([P, 4, P], F32, name="back")
+            for tt in range(4):
+                cols = slice(tt * P, (tt + 1) * P)
+                nc.tensor.matmul(out=back[:, tt, :], lhsT=uv[:, 0, cols], rhs=ident[:], start=True, stop=False, is_transpose=True)
+                nc.tensor.matmul(out=back[:, tt, :], lhsT=uv[:, 1, cols], rhs=perm[:], start=False, stop=True, is_transpose=True)
+            backs[n] = back
+
+        def leave(n):
+            o = outp.tile([P, 2, 2, P], F32, name="o")
+            src = backs[n][:].rearrange("p (b e) d -> p b e d", b=2)
+            nc.scalar.copy(out=o[:], in_=src)
+            dst = out_0 if n < 16 else out_1
+            nc.sync.dma_start(
+                out=dst[:, n % 16].rearrange("b (p e) d -> p b (e d)", e=2),
+                in_=o[:].rearrange("p b e d -> p b (e d)"),
+            )
+
+        with tc.manual_schedule():
+            load_w(0)
+            load_scales()
+            load_x(0, 0)
+            load_w(1)
+            load_x(0, 1)
+            load_x(1, 0)
+            load_w(2)
+            load_x(1, 1)
+            load_w(3)
+            load_tables()
+            for n in range(4, HEADS):
+                load_w(n)
+            constants()
+
+            cast(0, 2)
+            w_transposes(0, "acc")
+            w_out(0, 0)
+            w_out(0, 1)
+            cast(1, 2)
+            xb = {}
+            for g in range(2):
+                xb[(0, g)] = x_transposes(0, g)
+            for g in range(2):
+                x_out(0, g, xb[(0, g)])
+            w_transposes(1, "back")
+            w_quant(0)
+            w_out(1, 0)
+            w_out(1, 1)
+            for g in range(2, 4):
+                xb[(0, g)] = x_transposes(0, g)
+                x_out(0, g, xb[(0, g)])
+            for g in range(4):
+                xb[(1, g)] = x_transposes(1, g)
+                x_out(1, g, xb[(1, g)], on_vector=(g >= 2))
+            cast(2)
+            tu = tables()
+            tables_out(tu)
             x_quant(0)
             x_quant(1)
 
-            for i in range(NSTEP + 2):
-                if i >= 1 and i + 2 < NSTEP:
-                    casts(i + 2)
-                if i + 1 < NSTEP and 2 <= i:
-                    banks = transposes(w_halves(i + 1), lambda g: way_back(i - 2, g // 2, g % 2))
-                elif i + 1 < NSTEP:
-                    banks = transposes(w_halves(i + 1))
-                elif i == NSTEP - 1:
-                    for g in range(PASSES):
-                        way_back(i - 2, g // 2, g % 2)
-                    way_back(i - 1, 0, 0)
-                    way_back(i - 1, 0, 1)
-                elif i == NSTEP:
-                    way_back(i - 2, 1, 0)
-                    way_back(i - 2, 1, 1)
-                else:
-                    for g in range(PASSES):
-                        way_back(i - 2, g // 2, g % 2)
-                if i < NSTEP:
-                    products(i, 0)
-                    products(i, 1)
-                if i + 1 < NSTEP:
-                    w_out(i + 1, banks)
-                if 2 <= i:
-                    leave(i - 2, 1)
-                if i + 1 < NSTEP:
+            for i in range(HEADS + 4):
+                if i + 3 < HEADS:
+                    cast(i + 3)
+                if 0 <= i - 1 < HEADS and i - 1 not in ROT_ON_VECTOR:
+                    add_bias(i - 1)
+                    rotate_gpsimd(i - 1)
+                if i + 2 < HEADS:
+                    w_transposes(i + 2)
+                    w_out(i + 2, 0)
+                if 0 <= i - 3 < HEADS:
+                    way_back(i - 3)
+                if i + 1 < HEADS:
                     w_quant(i + 1)
-                if i < NSTEP:
-                    rotate_vector(i, 0)
-                    rotate_vector(i, 1)
-                if 2 <= i:
-                    leave(i - 2, 0)
-                if i < NSTEP:
-                    rotate_gpsimd(i, 0)
-                    rotate_gpsimd(i, 1)
+                if i + 2 < HEADS:
+                    w_out(i + 2, 1)
+                if i < HEADS:
+                    products(i)
+                if 0 <= i - 3 < HEADS:
+                    leave(i - 3)
+                if i < HEADS and i in ROT_ON_VECTOR:
+                    rotate_vector(i)

@@ -19,6 +19,7 @@ HEADS = 32
 FLOPS = 2 * 512 * 4096 * 2048
 
 ROT_ON_VECTOR = (30, 31)
+REORDERED = tuple(range(4, HEADS, 2))
 CAST_ON_VECTOR = (0,)
 
 
@@ -27,7 +28,8 @@ def tile_selfattention_pa_kernel(tc, x, Wqk_bytes, Wqk_scale, bqk, cos, sin, out
     with ExitStack() as ctx:
         const = ctx.enter_context(tc.tile_pool(name="const", bufs=1))
         wraw = ctx.enter_context(tc.tile_pool(name="wraw", bufs=HEADS))
-        wbp = ctx.enter_context(tc.tile_pool(name="wbp", bufs=5))
+        wbp = ctx.enter_context(tc.tile_pool(name="wbp", bufs=6))
+        wrp = ctx.enter_context(tc.tile_pool(name="wrp", bufs=3))
         wgp = ctx.enter_context(tc.tile_pool(name="wgp", bufs=3))
         wcp = ctx.enter_context(tc.tile_pool(name="wcp", bufs=3))
         uvp = ctx.enter_context(tc.tile_pool(name="uvp", bufs=5))
@@ -39,6 +41,7 @@ def tile_selfattention_pa_kernel(tc, x, Wqk_bytes, Wqk_scale, bqk, cos, sin, out
 
         wbys = {}
         wbs = {}
+        wrs = {}
         wgs = {}
         codes = {}
         accs = {}
@@ -120,6 +123,13 @@ def tile_selfattention_pa_kernel(tc, x, Wqk_bytes, Wqk_scale, bqk, cos, sin, out
                     nc.scalar.copy(out=wb[:, cols], in_=wbys[n][:, cols].bitcast(FP8))
             wbs[n] = wb
 
+        def reorder(n):
+            if n not in REORDERED:
+                return
+            wr = wrp.tile([P, 2, PASSES * P], F32, name="wr")
+            nc.scalar.copy(out=wr[:], in_=wbs[n][:].bitcast(F32).rearrange("p (w u) -> p u w", u=2))
+            wrs[n] = wr
+
         def new_bank(pool):
             if pool == "tp":
                 return tpp.tile([P, 2, 256], F32, name="tp")[:]
@@ -134,8 +144,12 @@ def tile_selfattention_pa_kernel(tc, x, Wqk_bytes, Wqk_scale, bqk, cos, sin, out
                 tp = new_bank(pool)
                 for u in range(2):
                     for gg in range(2):
-                        w0 = 256 * (2 * gp + gg)
-                        nc.tensor.transpose(tp[:, u, gg * P : (gg + 1) * P], words[:, w0 + u : w0 + 256 : 2], ident[:])
+                        g = 2 * gp + gg
+                        if n in REORDERED:
+                            src = wrs[n][:, u, g * P : (g + 1) * P]
+                        else:
+                            src = words[:, 256 * g + u : 256 * (g + 1) : 2]
+                        nc.tensor.transpose(tp[:, u, gg * P : (gg + 1) * P], src, ident[:])
                 w_banks[n].append(tp)
 
         def x_transposes(b, g, pool="tp"):
@@ -296,14 +310,17 @@ def tile_selfattention_pa_kernel(tc, x, Wqk_bytes, Wqk_scale, bqk, cos, sin, out
             x_quant(0)
             x_quant(1)
 
+            cast(3)
+
             for i in range(HEADS + 4):
-                if i + 3 < HEADS:
-                    cast(i + 3)
                 if 0 <= i - 1 < HEADS and i - 1 not in ROT_ON_VECTOR:
                     add_bias(i - 1)
                     rotate_gpsimd(i - 1)
+                if i + 3 < HEADS:
+                    reorder(i + 3)
                 if i + 2 < HEADS:
                     w_transposes(i + 2)
+                if i + 2 < HEADS:
                     w_out(i + 2, 0)
                 if 0 <= i - 3 < HEADS:
                     way_back(i - 3)
@@ -311,9 +328,11 @@ def tile_selfattention_pa_kernel(tc, x, Wqk_bytes, Wqk_scale, bqk, cos, sin, out
                     w_quant(i + 1)
                 if i + 2 < HEADS:
                     w_out(i + 2, 1)
-                if i < HEADS:
-                    products(i)
                 if 0 <= i - 3 < HEADS:
                     leave(i - 3)
+                if i + 4 < HEADS:
+                    cast(i + 4)
+                if i < HEADS:
+                    products(i)
                 if i < HEADS and i in ROT_ON_VECTOR:
                     rotate_vector(i)

from contextlib import ExitStack

import concourse.mybir as mybir
from concourse.masks import make_identity

F32 = mybir.dt.float32
BF16 = mybir.dt.bfloat16
U32 = mybir.dt.uint32
U8 = mybir.dt.uint8
FP8 = mybir.dt.float8_e4m3fn
FP8X4 = mybir.dt.float8_e4m3fn_x4
ALU = mybir.AluOpType
ACT = mybir.ActivationFunctionType

P = 128
K = 2048
PASSES = 4
HEADS = 32
FLOPS = 2 * 512 * 4096 * 2048

ROT_ON_VECTOR = (30, 31)
REORDERED = tuple(range(4, HEADS, 2))
CAST_ON_VECTOR = (0,)


def tile_selfattention_pa_kernel(tc, x, Wqk_bytes, Wqk_scale, bqk, cos, sin, out_0, out_1):
    nc = tc.nc
    with ExitStack() as ctx:
        const = ctx.enter_context(tc.tile_pool(name="const", bufs=1))
        wraw = ctx.enter_context(tc.tile_pool(name="wraw", bufs=HEADS))
        wbp = ctx.enter_context(tc.tile_pool(name="wbp", bufs=6))
        wrp = ctx.enter_context(tc.tile_pool(name="wrp", bufs=3))
        wgp = ctx.enter_context(tc.tile_pool(name="wgp", bufs=3))
        wcp = ctx.enter_context(tc.tile_pool(name="wcp", bufs=3))
        uvp = ctx.enter_context(tc.tile_pool(name="uvp", bufs=5))
        ytp = ctx.enter_context(tc.tile_pool(name="ytp", bufs=3))
        outp = ctx.enter_context(tc.tile_pool(name="outp", bufs=6))
        tpp = ctx.enter_context(tc.psum_pool(name="tpp", bufs=4))
        accp = ctx.enter_context(tc.psum_pool(name="accp", bufs=2))
        backp = ctx.enter_context(tc.psum_pool(name="backp", bufs=2))

        wbys = {}
        wbs = {}
        wrs = {}
        wgs = {}
        codes = {}
        accs = {}
        uvs = {}
        backs = {}
        w_banks = {}

        x_sb = {}
        for b in range(2):
            for half in range(2):
                x_sb[(b, half)] = const.tile([P, 2, 1024], BF16, name="x_sb%d%d" % (b, half))
        sc4 = const.tile([P, PASSES, 4], F32, name="sc4")
        cos_sb = const.tile([P, 2, 64], BF16, name="cos_sb")
        sin_sb = const.tile([P, 2, 64], BF16, name="sin_sb")
        brow_bf = const.tile([32, P], BF16, name="brow_bf")
        brow = const.tile([P, P], F32, name="brow")
        biasc = const.tile([P, 32], F32, name="biasc")
        ident = const.tile([P, P], F32, name="ident")
        perm = const.tile([P, P], F32, name="perm")
        nat = const.tile([P, 2, 2, 2, 64], F32, name="nat")
        tabs = const.tile([P, 2, 256], F32, name="tabs")
        xg = const.tile([P, PASSES, 512, 4], BF16, name="xg", align_bytes=64)
        xc = const.tile([P, PASSES, 512], U32, name="xc", align_bytes=64)
        xs = const.tile([P, PASSES, 512], U8, name="xs", align_bytes=64)

        def load_x(b, half):
            nc.sync.dma_start(
                out=x_sb[(b, half)][:],
                in_=x[b].rearrange("(p e) k -> p e k", e=2)[:, :, 1024 * half : 1024 * (half + 1)],
            )

        def load_w(n):
            wby = wraw.tile([P, K], U8, name="wby")
            nc.sync.dma_start(out=wby[:], in_=Wqk_bytes[P * n : P * (n + 1), :])
            wbys[n] = wby

        make_identity(nc, ident[:])

        def load_scales():
            nc.sync.dma_start(out=sc4[:], in_=Wqk_scale.rearrange("o (g p t) -> p (o g) t", p=P, t=4))

        def load_tables():
            nc.sync.dma_start(out=cos_sb[:], in_=cos.rearrange("(p e) i -> p e i", e=2))
            nc.sync.dma_start(out=sin_sb[:], in_=sin.rearrange("(p e) i -> p e i", e=2))
            nc.sync.dma_start(out=brow_bf[:], in_=bqk.rearrange("(j p) -> j p", p=P))

        def constants():
            nc.gpsimd.tensor_copy(out=perm[:, 0:64], in_=ident[:, 64:128])
            nc.gpsimd.tensor_copy(out=perm[:, 64:128], in_=ident[:, 0:64])
            nc.gpsimd.memset(brow[:], 0.0)
            nc.gpsimd.tensor_copy(out=nat[:, 0], in_=cos_sb[:].unsqueeze(2).to_broadcast([P, 2, 2, 64]))
            nc.gpsimd.tensor_copy(out=nat[:, 1, :, 0, :], in_=sin_sb[:])
            nc.gpsimd.tensor_scalar(out=nat[:, 1, :, 1, :], in0=sin_sb[:], scalar1=-1.0, scalar2=0.0, op0=ALU.mult, op1=ALU.add)
            nc.gpsimd.tensor_copy(out=brow[0:32, :], in_=brow_bf[:])

        def tables():
            tb = tpp.tile([P, 2, 256], F32, name="tp")
            tbv = tb[:].rearrange("p a (b c) -> p (a b) c", b=2)
            natv = nat[:].rearrange("p s e a i -> p (s e) (a i)")
            for q in range(4):
                nc.tensor.transpose(tbv[:, q, :], natv[:, q, :], ident[:])
            bb = tpp.tile([P, 2, 256], F32, name="tp")
            nc.tensor.transpose(bb[:, 0, 0:P], brow[:], ident[:])
            return tb, bb

        def tables_out(banks):
            tb, bb = banks
            nc.scalar.copy(out=biasc[:], in_=bb[:, 0, 0:32])
            nc.scalar.copy(out=tabs[:].rearrange("p s t -> p (s t)"), in_=tb[:].rearrange("p a c -> p (a c)"))

        def cast(n, parts=1):
            wb = wbp.tile([P, K], BF16, name="wb")
            width = K // parts
            for part in range(parts):
                cols = slice(width * part, width * (part + 1))
                if n in CAST_ON_VECTOR:
                    nc.vector.tensor_copy(out=wb[:, cols], in_=wbys[n][:, cols].bitcast(FP8))
                else:
                    nc.scalar.copy(out=wb[:, cols], in_=wbys[n][:, cols].bitcast(FP8))
            wbs[n] = wb

        def reorder(n):
            if n not in REORDERED:
                return
            wr = wrp.tile([P, 2, PASSES * P], F32, name="wr")
            nc.scalar.copy(out=wr[:], in_=wbs[n][:].bitcast(F32).rearrange("p (w u) -> p u w", u=2))
            wrs[n] = wr

        def new_bank(pool):
            if pool == "tp":
                return tpp.tile([P, 2, 256], F32, name="tp")[:]
            if pool == "acc":
                return accp.tile([P, 512], F32, name="acc")[:].rearrange("p (u r) -> p u r", u=2)
            return backp.tile([P, 4, P], F32, name="back")[:].rearrange("p (u c) d -> p u (c d)", u=2)

        def w_transposes(n, pool="tp"):
            words = wbs[n][:].bitcast(F32)
            w_banks[n] = []
            for gp in range(2):
                tp = new_bank(pool)
                for u in range(2):
                    for gg in range(2):
                        g = 2 * gp + gg
                        if n in REORDERED:
                            src = wrs[n][:, u, g * P : (g + 1) * P]
                        else:
                            src = words[:, 256 * g + u : 256 * (g + 1) : 2]
                        nc.tensor.transpose(tp[:, u, gg * P : (gg + 1) * P], src, ident[:])
                w_banks[n].append(tp)

        def x_transposes(b, g, pool="tp"):
            words = x_sb[(b, g // 2)][:].bitcast(F32)
            w0 = 256 * (g % 2)
            tp = new_bank(pool)
            for u in range(2):
                for e in range(2):
                    nc.tensor.transpose(tp[:, u, e * P : (e + 1) * P], words[:, e, w0 + u : w0 + 256 : 2], ident[:])
            return tp

        def x_out(b, g, bank, on_vector=False):
            dst_words = (
                xg[:, g, 256 * b : 256 * (b + 1), :]
                .rearrange("p r t -> p (r t)")
                .bitcast(F32)
                .rearrange("p (r u) -> p r u", u=2)
            )
            src = bank.rearrange("p u r -> p r u")
            if on_vector:
                nc.vector.tensor_copy(out=dst_words, in_=src)
            else:
                nc.scalar.copy(out=dst_words, in_=src)

        def x_quant(gp):
            nc.vector.quantize_mx(
                out=xc[:, 2 * gp : 2 * gp + 2, :].rearrange("p g n -> p (g n)").bitcast(FP8X4),
                scales=xs[:, 2 * gp : 2 * gp + 2, :].rearrange("p g n -> p (g n)"),
                in_=xg[:, 2 * gp : 2 * gp + 2].rearrange("p g n t -> p (g n t)"),
            )

        def w_out(n, gp):
            if gp == 0:
                wgs[n] = wgp.tile([P, PASSES, P, 4], BF16, name="wg", align_bytes=64)
            nc.vector.tensor_tensor(
                out=wgs[n][:, 2 * gp : 2 * gp + 2].rearrange("p g r (u e) -> p g r u e", u=2),
                in0=w_banks[n][gp].bitcast(BF16).rearrange("p u (g r e) -> p g r u e", g=2, e=2),
                in1=sc4[:, 2 * gp : 2 * gp + 2, :]
                .rearrange("p g (u e) -> p g u e", u=2)
                .unsqueeze(2)
                .to_broadcast([P, 2, P, 2, 2]),
                op=ALU.mult,
            )

        def w_quant(n):
            wc = wcp.tile([P, PASSES, P], U32, name="wc", align_bytes=64)
            ws = wcp.tile([P, PASSES, P], U8, name="ws", align_bytes=64)
            nc.vector.quantize_mx(
                out=wc[:].rearrange("p g n -> p (g n)").bitcast(FP8X4),
                scales=ws[:].rearrange("p g n -> p (g n)"),
                in_=wgs[n][:].rearrange("p g n t -> p (g n t)"),
            )
            codes[n] = (wc, ws)

        def products(n):
            wc, ws = codes[n]
            acc = accp.tile([P, 512], F32, name="acc")
            for g in range(PASSES):
                nc.tensor.matmul_mx(
                    out=acc[:],
                    lhsT=wc[:, g, :].bitcast(FP8X4),
                    lhsT_scale=ws[:, g, :],
                    rhs=xc[:, g, :].bitcast(FP8X4),
                    rhs_scale=xs[:, g, :],
                    start=(g == 0),
                    stop=(g == PASSES - 1),
                )
            accs[n] = acc

        def table(cs):
            return tabs[:, cs, :].unsqueeze(1).to_broadcast([P, 2, 256])

        def rotate_vector(n):
            uv = uvp.tile([P, 2, 512], F32, name="uv")
            for cs in range(2):
                nc.vector.scalar_tensor_tensor(
                    out=uv[:, cs, :].rearrange("p (b t) -> p b t", b=2),
                    in0=accs[n][:].rearrange("p (b t) -> p b t", b=2),
                    scalar=biasc[:, n : n + 1],
                    in1=table(cs),
                    op0=ALU.add,
                    op1=ALU.mult,
                )
            uvs[n] = uv

        def add_bias(n):
            yt = ytp.tile([P, 512], F32, name="yt")
            nc.scalar.activation(out=yt[:], in_=accs[n][:], func=ACT.Identity, bias=biasc[:, n : n + 1])
            uvs[n] = yt

        def rotate_gpsimd(n):
            uv = uvp.tile([P, 2, 512], F32, name="uv")
            nc.gpsimd.tensor_tensor(
                out=uv[:].rearrange("p s (b t) -> p s b t", b=2),
                in0=uvs[n][:].rearrange("p (b t) -> p b t", b=2).unsqueeze(1).to_broadcast([P, 2, 2, 256]),
                in1=tabs[:].unsqueeze(2).to_broadcast([P, 2, 2, 256]),
                op=ALU.mult,
            )
            uvs[n] = uv

        def way_back(n):
            uv = uvs[n]
            back = backp.tile([P, 4, P], F32, name="back")
            for tt in range(4):
                cols = slice(tt * P, (tt + 1) * P)
                nc.tensor.matmul(out=back[:, tt, :], lhsT=uv[:, 0, cols], rhs=ident[:], start=True, stop=False, is_transpose=True)
                nc.tensor.matmul(out=back[:, tt, :], lhsT=uv[:, 1, cols], rhs=perm[:], start=False, stop=True, is_transpose=True)
            backs[n] = back

        def leave(n):
            o = outp.tile([P, 2, 2, P], F32, name="o")
            src = backs[n][:].rearrange("p (b e) d -> p b e d", b=2)
            nc.scalar.copy(out=o[:], in_=src)
            dst = out_0 if n < 16 else out_1
            nc.sync.dma_start(
                out=dst[:, n % 16].rearrange("b (p e) d -> p b (e d)", e=2),
                in_=o[:].rearrange("p b e d -> p b (e d)"),
            )

        with tc.manual_schedule():
            load_w(0)
            load_scales()
            load_x(0, 0)
            load_w(1)
            load_x(0, 1)
            load_x(1, 0)
            load_w(2)
            load_x(1, 1)
            load_w(3)
            load_tables()
            for n in range(4, HEADS):
                load_w(n)
            constants()

            cast(0, 2)
            w_transposes(0, "acc")
            w_out(0, 0)
            w_out(0, 1)
            cast(1, 2)
            xb = {}
            for g in range(2):
                xb[(0, g)] = x_transposes(0, g)
            for g in range(2):
                x_out(0, g, xb[(0, g)])
            w_transposes(1, "back")
            w_quant(0)
            w_out(1, 0)
            w_out(1, 1)
            for g in range(2, 4):
                xb[(0, g)] = x_transposes(0, g)
                x_out(0, g, xb[(0, g)])
            for g in range(4):
                xb[(1, g)] = x_transposes(1, g)
                x_out(1, g, xb[(1, g)], on_vector=(g >= 2))
            cast(2)
            tu = tables()
            tables_out(tu)
            x_quant(0)
            x_quant(1)

            cast(3)

            for i in range(HEADS + 4):
                if 0 <= i - 1 < HEADS and i - 1 not in ROT_ON_VECTOR:
                    add_bias(i - 1)
                    rotate_gpsimd(i - 1)
                if i + 3 < HEADS:
                    reorder(i + 3)
                if i + 2 < HEADS:
                    w_transposes(i + 2)
                if i + 2 < HEADS:
                    w_out(i + 2, 0)
                if 0 <= i - 3 < HEADS:
                    way_back(i - 3)
                if i + 1 < HEADS:
                    w_quant(i + 1)
                if i + 2 < HEADS:
                    w_out(i + 2, 1)
                if 0 <= i - 3 < HEADS:
                    leave(i - 3)
                if i + 4 < HEADS:
                    cast(i + 4)
                if i < HEADS:
                    products(i)
                if i < HEADS and i in ROT_ON_VECTOR:
                    rotate_vector(i)
